import numpy as np
import ml_dtypes


def mxq(x, axis, fmt="e4m3"):
    dtype, down = {"e4m3": (ml_dtypes.float8_e4m3fn, 7), "e5m2": (ml_dtypes.float8_e5m2, 14)}[fmt]
    v = np.moveaxis(np.asarray(x, np.float32).astype(ml_dtypes.bfloat16).astype(np.float64), axis, -1)
    blocks = v.reshape(v.shape[:-1] + (-1, 32))
    amax = np.abs(blocks).max(-1, keepdims=True)
    byte = np.maximum(np.where(amax > 0, np.frexp(amax)[1] - 1 + 127, 0) - down, 1)
    scale = np.exp2(byte - 127.0)
    codes = (blocks / scale).astype(np.float32).astype(dtype).astype(np.float64)
    return np.moveaxis((codes * scale).reshape(v.shape), -1, axis)


WIDE = False


def mx_kscale(k):
    if not WIDE:
        return np.ones(k)
    levels = np.array([20, -20, 10, -10, 0])
    a = np.random.permutation(np.resize(levels, k // 512 * 4)).reshape(k // 512, 4)
    idx = np.arange(k)
    return np.exp2(a[idx // 512, idx % 128 // 32])


BF16 = ml_dtypes.bfloat16


def bf(x):
    return np.asarray(x, np.float32).astype(BF16)


def f64(x):
    return np.asarray(x).astype(np.float64)


N, C, O, OH, OW, KH, KW, STRIDE, PAD = 512, 128, 512, 3, 2, 3, 3, 1, 1
H, W = (OH - 1) * STRIDE + KH - 2 * PAD, (OW - 1) * STRIDE + KW - 2 * PAD
NEG_SLOPE = 0.1


def span(t, n_out, n_in):
    ok = [p for p in range(n_out) if 0 <= p * STRIDE + t - PAD < n_in]
    return ok[0], ok[-1] + 1


def preact(x, weight, bias):
    xf, wt = f64(x), f64(weight)[0]
    acc = np.zeros((N, O, OH, OW))
    for i in range(KH):
        h0, h1 = span(i, OH, H)
        a0 = h0 * STRIDE + i - PAD
        for j in range(KW):
            w0, w1 = span(j, OW, W)
            b0 = w0 * STRIDE + j - PAD
            xs = xf[:, :, a0:a0 + (h1 - h0 - 1) * STRIDE + 1:STRIDE, b0:b0 + (w1 - w0 - 1) * STRIDE + 1:STRIDE]
            ws = wt[:, :, h0:h1, w0:w1, i * KW + j]
            p = xs.transpose(2, 3, 0, 1) @ ws.transpose(2, 3, 1, 0)
            acc[:, :, h0:h1, w0:w1] += p.transpose(2, 3, 0, 1)
    return acc + f64(bias)


def setup_inputs():
    s = mx_kscale(N)[:, None, None, None]
    x0 = bf(np.random.standard_normal((N, C, H, W)))
    weight = bf(np.random.standard_normal((1, O, C, OH, OW, KH * KW)) * np.sqrt(2.0 / (KH * KW * C)))
    bias = bf(np.random.standard_normal((1, O, OH, OW)) * 0.3)
    g = np.random.standard_normal((N, O, OH, OW)) * np.exp2(np.random.randint(-12, 1, (N, 1, 1, 1))) / s
    z = preact(x0, weight, bias)
    g = g * (np.abs(z) >= 1e-4)
    return {"x": bf(f64(x0) * s), "weight": weight, "bias": bias, "z": np.asarray(z, np.float32), "grad_out": bf(g)}


def reference(x, weight, bias, z, grad_out):
    dz = f64(grad_out) * np.where(f64(z) >= 0, 1.0, NEG_SLOPE)
    dq = mxq(dz, 0, "e5m2")
    xq = mxq(f64(x), 0, "e4m3")
    gw = np.zeros((1, O, C, OH, OW, KH * KW))
    for i in range(KH):
        h0, h1 = span(i, OH, H)
        a0 = h0 * STRIDE + i - PAD
        for j in range(KW):
            w0, w1 = span(j, OW, W)
            b0 = w0 * STRIDE + j - PAD
            xs = xq[:, :, a0:a0 + (h1 - h0 - 1) * STRIDE + 1:STRIDE, b0:b0 + (w1 - w0 - 1) * STRIDE + 1:STRIDE]
            ds = dq[:, :, h0:h1, w0:w1]
            p = ds.transpose(2, 3, 1, 0) @ xs.transpose(2, 3, 0, 1)
            gw[0, :, :, h0:h1, w0:w1, i * KW + j] = p.transpose(2, 3, 0, 1)
    return gw

@@ -1,0 +1,161 @@
+from contextlib import ExitStack
+
+import concourse.mybir as mybir
+
+F32 = mybir.dt.float32
+BF16 = mybir.dt.bfloat16
+U32 = mybir.dt.uint32
+U8 = mybir.dt.uint8
+I32 = mybir.dt.int32
+E4M3_X4 = mybir.dt.float8_e4m3fn_x4
+E5M2_X4 = mybir.dt.float8_e5m2_x4
+ALU = mybir.AluOpType
+
+BATCH, C, O, OH, OW, KH, KW = 512, 128, 512, 3, 2, 3, 3
+XH, XW = 3, 2
+NEG_SLOPE = 0.1
+
+P = 128
+PACK = 4
+assert BATCH == P * PACK
+
+O_TILE = P
+O_TILES = O // O_TILE
+DZ_COLS = O_TILE * OH * OW
+X_COLS = C * XH * XW
+
+C_PART = 32
+C_PARTS = C // C_PART
+WINDOW_BLOCKS = 8
+WINDOW = WINDOW_BLOCKS * C_PART
+N_MOVING = 2 * WINDOW
+assert N_MOVING == 512
+WINDOWS = C_PARTS * OH
+WINDOWS_COLS = (2 * WINDOWS + 1) * WINDOW
+
+PER_C = OH * OW * KH * KW
+PER_H = OW * KH * KW
+OUT_COLS = C_PART * PER_C
+OUT_BUFS = 8
+PSUM_BANKS = 8
+
+FLOPS = 2 * 28 * O * BATCH * C
+BYTES = 2 * BATCH * X_COLS + (4 + 2) * BATCH * O * OH * OW + 4 * O * C * PER_C
+
+
+def tile_locallyconnected2d_v_kernel(tc, x, weight, bias, z, grad_out, out):
+    nc = tc.nc
+    with ExitStack() as pools:
+        keep = pools.enter_context(tc.tile_pool(name="keep", bufs=1))
+        loads = pools.enter_context(tc.tile_pool(name="loads", bufs=O_TILES))
+        work = pools.enter_context(tc.tile_pool(name="work", bufs=2))
+        banks = pools.enter_context(tc.psum_pool(name="banks", bufs=PSUM_BANKS))
+
+        win_codes = keep.tile([P, WINDOWS_COLS], U32, align_bytes=64)
+        win_scales = keep.tile([P, WINDOWS_COLS], U8, align_bytes=64)
+        nc.vector.memset(win_codes[:].bitcast(I32), 0)
+        nc.vector.memset(win_scales[:].bitcast(I32), 0)
+        x_scales = keep.tile([P, X_COLS], U8, align_bytes=64)
+        nc.vector.memset(x_scales[:].bitcast(I32), 0)
+        zero = keep.tile([P, 1], F32)
+        nc.vector.memset(zero[:], 0.0)
+        out_tiles = []
+        for i in range(OUT_BUFS):
+            out_tile = keep.tile([P, OUT_COLS], F32, name="out_tile%d" % i)
+            nc.scalar.copy(out=out_tile[:], in_=zero[:].to_broadcast([P, OUT_COLS]))
+            out_tiles.append(out_tile)
+
+        x_raw = keep.tile([P, PACK, X_COLS], BF16)
+        nc.sync.dma_start(out=x_raw[:], in_=x.rearrange("(p j) c r s -> p j (c r s)", j=PACK))
+        g_rows = grad_out.rearrange("(p j) o h w -> p j (o h w)", j=PACK)
+        z_rows = z.rearrange("(p j) o h w -> p j (o h w)", j=PACK)
+        g_raws = []
+        z_raws = []
+        for t in range(O_TILES):
+            dz_cols = slice(t * DZ_COLS, (t + 1) * DZ_COLS)
+            g_raw = loads.tile([P, PACK, DZ_COLS], BF16, name="g_raw")
+            nc.sync.dma_start(out=g_raw[:], in_=g_rows[:, :, dz_cols])
+            g_raws.append(g_raw)
+            z_raw = loads.tile([P, PACK, DZ_COLS], F32, name="z_raw")
+            nc.sync.dma_start(out=z_raw[:], in_=z_rows[:, :, dz_cols])
+            z_raws.append(z_raw)
+
+        x_grouped = keep.tile([P, X_COLS * PACK], BF16, align_bytes=64)
+        x_codes = keep.tile([P, X_COLS], U32, align_bytes=64)
+        x_from = x_raw[:].rearrange("p j (c r s) -> p r c s j", r=XH, s=XW)
+        x_to = x_grouped[:].rearrange("p (r s c j) -> p r c s j", r=XH, s=XW, j=PACK)
+        for r in range(XH):
+            nc.vector.tensor_copy(out=x_to[:, r], in_=x_from[:, r])
+        row_cols = XW * C
+        for r in range(XH):
+            cols = slice(r * row_cols, (r + 1) * row_cols)
+            nc.vector.quantize_mx(
+                out=x_codes[:, cols].bitcast(E4M3_X4),
+                scales=x_scales[:, cols],
+                in_=x_grouped[:, r * row_cols * PACK : (r + 1) * row_cols * PACK],
+            )
+
+        def place_row(windows, x_plane, block, h, i):
+            r = h + i - 1
+            row = x_plane[:, r * XW * C_PARTS * block : (r + 1) * XW * C_PARTS * block]
+            behind_first_zeros = windows[:, WINDOW_BLOCKS * block :]
+            window_h = behind_first_zeros.rearrange(
+                "p (q h e k c) -> p q h e k c", q=C_PARTS, h=OH, e=2, k=WINDOW_BLOCKS
+            )[:, :, h, 0]
+            nc.vector.tensor_copy(
+                out=window_h[:, :, KW * i : KW * i + XW, :],
+                in_=row.rearrange("p (s q c) -> p q s c", s=XW, q=C_PARTS),
+            )
+
+        for h in range(OH):
+            for i in range(KH):
+                if 0 <= h + i - 1 < XH:
+                    place_row(win_codes[:].bitcast(I32), x_codes[:].bitcast(I32), C_PART, h, i)
+                    place_row(win_scales[:].bitcast(I32), x_scales[:].bitcast(I32), C_PART // 4, h, i)
+
+        out_rows = out.rearrange("a (t o) c h w k -> (a t) o (c h w k)", o=O_TILE)
+        for t in range(O_TILES):
+            slope = z_raws[t]
+            nc.vector.tensor_scalar(
+                out=slope[:], in0=z_raws[t][:], scalar1=0.0, scalar2=NEG_SLOPE, op0=ALU.is_ge, op1=ALU.max
+            )
+            dz_grouped = work.tile([P, DZ_COLS * PACK], BF16, align_bytes=64)
+            dz_codes = work.tile([P, DZ_COLS], U32, align_bytes=64)
+            dz_scales = work.tile([P, DZ_COLS], U8, align_bytes=64)
+            slope_from = slope[:].rearrange("p j (o h w) -> p h o w j", h=OH, w=OW)
+            g_from = g_raws[t][:].rearrange("p j (o h w) -> p h o w j", h=OH, w=OW)
+            dz_to = dz_grouped[:].rearrange("p (h w o j) -> p h o w j", h=OH, w=OW, j=PACK)
+            for h in range(OH):
+                nc.vector.tensor_tensor(out=dz_to[:, h], in0=slope_from[:, h], in1=g_from[:, h], op=ALU.mult)
+            h_cols = OW * O_TILE
+            for h in range(OH):
+                cols = slice(h * h_cols, (h + 1) * h_cols)
+                nc.vector.quantize_mx(
+                    out=dz_codes[:, cols].bitcast(E5M2_X4),
+                    scales=dz_scales[:, cols],
+                    in_=dz_grouped[:, h * h_cols * PACK : (h + 1) * h_cols * PACK],
+                )
+
+            for q in range(C_PARTS):
+                out_tile = out_tiles[(t * C_PARTS + q) % OUT_BUFS]
+                per_c = out_tile[:].rearrange("p (c f) -> p c f", f=PER_C)
+                for h in range(OH):
+                    window_start = (2 * (q * OH + h) + 1) * WINDOW
+                    bank = banks.tile([P, N_MOVING], F32)
+                    for w in range(OW):
+                        moving = slice(window_start - w * WINDOW, window_start - w * WINDOW + N_MOVING)
+                        stationary = slice((h * OW + w) * O_TILE, (h * OW + w + 1) * O_TILE)
+                        nc.tensor.matmul_mx(
+                            out=bank[:],
+                            lhsT=dz_codes[:, stationary].bitcast(E5M2_X4),
+                            lhsT_scale=dz_scales[:, stationary],
+                            rhs=win_codes[:, moving].bitcast(E4M3_X4),
+                            rhs_scale=win_scales[:, moving],
+                            start=(w == 0),
+                            stop=(w == OW - 1),
+                        )
+                    nc.scalar.copy(
+                        out=per_c[:, :, h * PER_H + 1 : (h + 1) * PER_H - 1],
+                        in_=bank[:].rearrange("p (f c) -> p c f", c=C_PART),
+                    )
+                nc.sync.dma_start(out=out_rows[t][:, q * OUT_COLS : (q + 1) * OUT_COLS], in_=out_tile[:])

@@ -51,6 +51,8 @@ def tile_locallyconnected2d_v_kernel(tc, x, weight, bias, z, grad_out, out):
         work = pools.enter_context(tc.tile_pool(name="work", bufs=2))
         banks = pools.enter_context(tc.psum_pool(name="banks", bufs=PSUM_BANKS))
 
+        pools.enter_context(tc.manual_schedule())
+
         win_codes = keep.tile([P, WINDOWS_COLS], U32, align_bytes=64)
         win_scales = keep.tile([P, WINDOWS_COLS], U8, align_bytes=64)
         nc.vector.memset(win_codes[:].bitcast(I32), 0)
@@ -84,16 +86,21 @@ def tile_locallyconnected2d_v_kernel(tc, x, weight, bias, z, grad_out, out):
         x_codes = keep.tile([P, X_COLS], U32, align_bytes=64)
         x_from = x_raw[:].rearrange("p j (c r s) -> p r c s j", r=XH, s=XW)
         x_to = x_grouped[:].rearrange("p (r s c j) -> p r c s j", r=XH, s=XW, j=PACK)
-        for r in range(XH):
-            nc.vector.tensor_copy(out=x_to[:, r], in_=x_from[:, r])
         row_cols = XW * C
-        for r in range(XH):
+
+        def quantise_x_row(r):
             cols = slice(r * row_cols, (r + 1) * row_cols)
             nc.vector.quantize_mx(
                 out=x_codes[:, cols].bitcast(E4M3_X4),
                 scales=x_scales[:, cols],
                 in_=x_grouped[:, r * row_cols * PACK : (r + 1) * row_cols * PACK],
             )
+
+        for r in range(XH + 1):
+            if r < XH:
+                nc.vector.tensor_copy(out=x_to[:, r], in_=x_from[:, r])
+            if r > 0:
+                quantise_x_row(r - 1)
 
         def place_row(windows, x_plane, block, h, i):
             r = h + i - 1
@@ -114,6 +121,7 @@ def tile_locallyconnected2d_v_kernel(tc, x, weight, bias, z, grad_out, out):
                     place_row(win_scales[:].bitcast(I32), x_scales[:].bitcast(I32), C_PART // 4, h, i)
 
         out_rows = out.rearrange("a (t o) c h w k -> (a t) o (c h w k)", o=O_TILE)
+        h_cols = OW * O_TILE
         for t in range(O_TILES):
             slope = z_raws[t]
             nc.vector.tensor_scalar(
@@ -125,21 +133,19 @@ def tile_locallyconnected2d_v_kernel(tc, x, weight, bias, z, grad_out, out):
             slope_from = slope[:].rearrange("p j (o h w) -> p h o w j", h=OH, w=OW)
             g_from = g_raws[t][:].rearrange("p j (o h w) -> p h o w j", h=OH, w=OW)
             dz_to = dz_grouped[:].rearrange("p (h w o j) -> p h o w j", h=OH, w=OW, j=PACK)
-            for h in range(OH):
-                nc.vector.tensor_tensor(out=dz_to[:, h], in0=slope_from[:, h], in1=g_from[:, h], op=ALU.mult)
-            h_cols = OW * O_TILE
-            for h in range(OH):
-                cols = slice(h * h_cols, (h + 1) * h_cols)
-                nc.vector.quantize_mx(
-                    out=dz_codes[:, cols].bitcast(E5M2_X4),
-                    scales=dz_scales[:, cols],
-                    in_=dz_grouped[:, h * h_cols * PACK : (h + 1) * h_cols * PACK],
-                )
+            for h in range(OH + 1):
+                if h < OH:
+                    nc.vector.tensor_tensor(out=dz_to[:, h], in0=slope_from[:, h], in1=g_from[:, h], op=ALU.mult)
+                if h > 0:
+                    cols = slice((h - 1) * h_cols, h * h_cols)
+                    nc.vector.quantize_mx(
+                        out=dz_codes[:, cols].bitcast(E5M2_X4),
+                        scales=dz_scales[:, cols],
+                        in_=dz_grouped[:, (h - 1) * h_cols * PACK : h * h_cols * PACK],
+                    )
 
-            for q in range(C_PARTS):
-                out_tile = out_tiles[(t * C_PARTS + q) % OUT_BUFS]
-                per_c = out_tile[:].rearrange("p (c f) -> p c f", f=PER_C)
-                for h in range(OH):
+            for h in range(OH):
+                for q in range(C_PARTS):
                     window_start = (2 * (q * OH + h) + 1) * WINDOW
                     bank = banks.tile([P, N_MOVING], F32)
                     for w in range(OW):
@@ -154,8 +160,11 @@ def tile_locallyconnected2d_v_kernel(tc, x, weight, bias, z, grad_out, out):
                             start=(w == 0),
                             stop=(w == OW - 1),
                         )
+                    out_tile = out_tiles[(t * C_PARTS + q) % OUT_BUFS]
+                    per_c = out_tile[:].rearrange("p (c f) -> p c f", f=PER_C)
                     nc.scalar.copy(
                         out=per_c[:, :, h * PER_H + 1 : (h + 1) * PER_H - 1],
                         in_=bank[:].rearrange("p (f c) -> p c f", c=C_PART),
                     )
-                nc.sync.dma_start(out=out_rows[t][:, q * OUT_COLS : (q + 1) * OUT_COLS], in_=out_tile[:])
+                    if h == OH - 1:
+                        nc.sync.dma_start(out=out_rows[t][:, q * OUT_COLS : (q + 1) * OUT_COLS], in_=out_tile[:])

@@ -53,12 +53,6 @@ def tile_locallyconnected2d_v_kernel(tc, x, weight, bias, z, grad_out, out):
 
         pools.enter_context(tc.manual_schedule())
 
-        win_codes = keep.tile([P, WINDOWS_COLS], U32, align_bytes=64)
-        win_scales = keep.tile([P, WINDOWS_COLS], U8, align_bytes=64)
-        nc.vector.memset(win_codes[:].bitcast(I32), 0)
-        nc.vector.memset(win_scales[:].bitcast(I32), 0)
-        x_scales = keep.tile([P, X_COLS], U8, align_bytes=64)
-        nc.vector.memset(x_scales[:].bitcast(I32), 0)
         zero = keep.tile([P, 1], F32)
         nc.vector.memset(zero[:], 0.0)
         out_tiles = []
@@ -66,6 +60,12 @@ def tile_locallyconnected2d_v_kernel(tc, x, weight, bias, z, grad_out, out):
             out_tile = keep.tile([P, OUT_COLS], F32, name="out_tile%d" % i)
             nc.scalar.copy(out=out_tile[:], in_=zero[:].to_broadcast([P, OUT_COLS]))
             out_tiles.append(out_tile)
+        win_codes = keep.tile([P, WINDOWS_COLS], U32, align_bytes=64)
+        win_scales = keep.tile([P, WINDOWS_COLS], U8, align_bytes=64)
+        nc.vector.memset(win_codes[:].bitcast(I32), 0)
+        nc.vector.memset(win_scales[:].bitcast(I32), 0)
+        x_scales = keep.tile([P, X_COLS], U8, align_bytes=64)
+        nc.vector.memset(x_scales[:].bitcast(I32), 0)
 
         x_raw = keep.tile([P, PACK, X_COLS], BF16)
         nc.sync.dma_start(out=x_raw[:], in_=x.rearrange("(p j) c r s -> p j (c r s)", j=PACK))
@@ -144,8 +144,10 @@ def tile_locallyconnected2d_v_kernel(tc, x, weight, bias, z, grad_out, out):
                         in_=dz_grouped[:, (h - 1) * h_cols * PACK : h * h_cols * PACK],
                     )
 
-            for h in range(OH):
-                for q in range(C_PARTS):
+            for q in range(C_PARTS):
+                out_tile = out_tiles[(t * C_PARTS + q) % OUT_BUFS]
+                per_c = out_tile[:].rearrange("p (c f) -> p c f", f=PER_C)
+                for h in range(OH):
                     window_start = (2 * (q * OH + h) + 1) * WINDOW
                     bank = banks.tile([P, N_MOVING], F32)
                     for w in range(OW):
@@ -160,11 +162,10 @@ def tile_locallyconnected2d_v_kernel(tc, x, weight, bias, z, grad_out, out):
                             start=(w == 0),
                             stop=(w == OW - 1),
                         )
-                    out_tile = out_tiles[(t * C_PARTS + q) % OUT_BUFS]
-                    per_c = out_tile[:].rearrange("p (c f) -> p c f", f=PER_C)
+                    lead = KW * max(0, 1 - h)
+                    trail = KW * max(0, h + 2 - XH)
                     nc.scalar.copy(
-                        out=per_c[:, :, h * PER_H + 1 : (h + 1) * PER_H - 1],
-                        in_=bank[:].rearrange("p (f c) -> p c f", c=C_PART),
+                        out=per_c[:, :, h * PER_H + 1 + lead : (h + 1) * PER_H - 1 - trail],
+                        in_=bank[:].rearrange("p (f c) -> p c f", c=C_PART)[:, :, lead : 2 * WINDOW_BLOCKS - trail],
                     )
-                    if h == OH - 1:
-                        nc.sync.dma_start(out=out_rows[t][:, q * OUT_COLS : (q + 1) * OUT_COLS], in_=out_tile[:])
+                nc.sync.dma_start(out=out_rows[t][:, q * OUT_COLS : (q + 1) * OUT_COLS], in_=out_tile[:])

@@ -21,6 +21,7 @@ assert BATCH == P * PACK
 
 O_TILE = P
 O_TILES = O // O_TILE
+LOAD_GROUPS = ((0, 1), (1, 1), (2, 2))
 DZ_COLS = O_TILE * OH * OW
 X_COLS = C * XH * XW
 
@@ -47,7 +48,6 @@ def tile_locallyconnected2d_v_kernel(tc, x, weight, bias, z, grad_out, out):
     nc = tc.nc
     with ExitStack() as pools:
         keep = pools.enter_context(tc.tile_pool(name="keep", bufs=1))
-        loads = pools.enter_context(tc.tile_pool(name="loads", bufs=O_TILES))
         work = pools.enter_context(tc.tile_pool(name="work", bufs=2))
         banks = pools.enter_context(tc.psum_pool(name="banks", bufs=PSUM_BANKS))
 
@@ -73,14 +73,15 @@ def tile_locallyconnected2d_v_kernel(tc, x, weight, bias, z, grad_out, out):
         z_rows = z.rearrange("(p j) o h w -> p j (o h w)", j=PACK)
         g_raws = []
         z_raws = []
-        for t in range(O_TILES):
-            dz_cols = slice(t * DZ_COLS, (t + 1) * DZ_COLS)
-            g_raw = loads.tile([P, PACK, DZ_COLS], BF16, name="g_raw")
+        for first, count in LOAD_GROUPS:
+            dz_cols = slice(first * DZ_COLS, (first + count) * DZ_COLS)
+            g_raw = keep.tile([P, PACK, count * DZ_COLS], BF16, name="g_raw%d" % first)
             nc.sync.dma_start(out=g_raw[:], in_=g_rows[:, :, dz_cols])
-            g_raws.append(g_raw)
-            z_raw = loads.tile([P, PACK, DZ_COLS], F32, name="z_raw")
+            z_raw = keep.tile([P, PACK, count * DZ_COLS], F32, name="z_raw%d" % first)
             nc.sync.dma_start(out=z_raw[:], in_=z_rows[:, :, dz_cols])
-            z_raws.append(z_raw)
+            for i in range(count):
+                g_raws.append(g_raw[:, :, i * DZ_COLS : (i + 1) * DZ_COLS])
+                z_raws.append(z_raw[:, :, i * DZ_COLS : (i + 1) * DZ_COLS])
 
         x_grouped = keep.tile([P, X_COLS * PACK], BF16, align_bytes=64)
         x_codes = keep.tile([P, X_COLS], U32, align_bytes=64)
@@ -125,13 +126,13 @@ def tile_locallyconnected2d_v_kernel(tc, x, weight, bias, z, grad_out, out):
         for t in range(O_TILES):
             slope = z_raws[t]
             nc.vector.tensor_scalar(
-                out=slope[:], in0=z_raws[t][:], scalar1=0.0, scalar2=NEG_SLOPE, op0=ALU.is_ge, op1=ALU.max
+                out=slope, in0=z_raws[t], scalar1=0.0, scalar2=NEG_SLOPE, op0=ALU.is_ge, op1=ALU.max
             )
             dz_grouped = work.tile([P, DZ_COLS * PACK], BF16, align_bytes=64)
             dz_codes = work.tile([P, DZ_COLS], U32, align_bytes=64)
             dz_scales = work.tile([P, DZ_COLS], U8, align_bytes=64)
-            slope_from = slope[:].rearrange("p j (o h w) -> p h o w j", h=OH, w=OW)
-            g_from = g_raws[t][:].rearrange("p j (o h w) -> p h o w j", h=OH, w=OW)
+            slope_from = slope.rearrange("p j (o h w) -> p h o w j", h=OH, w=OW)
+            g_from = g_raws[t].rearrange("p j (o h w) -> p h o w j", h=OH, w=OW)
             dz_to = dz_grouped[:].rearrange("p (h w o j) -> p h o w j", h=OH, w=OW, j=PACK)
             for h in range(OH + 1):
                 if h < OH:

@@ -165,8 +165,10 @@ def tile_locallyconnected2d_v_kernel(tc, x, weight, bias, z, grad_out, out):
                         )
                     lead = KW * max(0, 1 - h)
                     trail = KW * max(0, h + 2 - XH)
-                    nc.scalar.copy(
-                        out=per_c[:, :, h * PER_H + 1 + lead : (h + 1) * PER_H - 1 - trail],
-                        in_=bank[:].rearrange("p (f c) -> p c f", c=C_PART)[:, :, lead : 2 * WINDOW_BLOCKS - trail],
-                    )
+                    to = per_c[:, :, h * PER_H + 1 + lead : (h + 1) * PER_H - 1 - trail]
+                    positions = bank[:].rearrange("p (f c) -> p c f", c=C_PART)[:, :, lead : 2 * WINDOW_BLOCKS - trail]
+                    if t == O_TILES - 1 and (q * OH + h) % 2 == 1:
+                        nc.vector.tensor_copy(out=to, in_=positions)
+                    else:
+                        nc.scalar.copy(out=to, in_=positions)
                 nc.sync.dma_start(out=out_rows[t][:, q * OUT_COLS : (q + 1) * OUT_COLS], in_=out_tile[:])

@@ -131,9 +131,9 @@ def tile_locallyconnected2d_v_kernel(tc, x, weight, bias, z, grad_out, out):
             dz_grouped = work.tile([P, DZ_COLS * PACK], BF16, align_bytes=64)
             dz_codes = work.tile([P, DZ_COLS], U32, align_bytes=64)
             dz_scales = work.tile([P, DZ_COLS], U8, align_bytes=64)
-            slope_from = slope.rearrange("p j (o h w) -> p h o w j", h=OH, w=OW)
-            g_from = g_raws[t].rearrange("p j (o h w) -> p h o w j", h=OH, w=OW)
-            dz_to = dz_grouped[:].rearrange("p (h w o j) -> p h o w j", h=OH, w=OW, j=PACK)
+            slope_from = slope.rearrange("p j (o h w) -> p h o j w", h=OH, w=OW)
+            g_from = g_raws[t].rearrange("p j (o h w) -> p h o j w", h=OH, w=OW)
+            dz_to = dz_grouped[:].rearrange("p (h w o j) -> p h o j w", h=OH, w=OW, j=PACK)
             for h in range(OH + 1):
                 if h < OH:
                     nc.vector.tensor_tensor(out=dz_to[:, h], in0=slope_from[:, h], in1=g_from[:, h], op=ALU.mult)

from contextlib import ExitStack

import concourse.mybir as mybir

F32 = mybir.dt.float32
BF16 = mybir.dt.bfloat16
U32 = mybir.dt.uint32
U8 = mybir.dt.uint8
I32 = mybir.dt.int32
E4M3_X4 = mybir.dt.float8_e4m3fn_x4
E5M2_X4 = mybir.dt.float8_e5m2_x4
ALU = mybir.AluOpType

BATCH, C, O, OH, OW, KH, KW = 512, 128, 512, 3, 2, 3, 3
XH, XW = 3, 2
NEG_SLOPE = 0.1

P = 128
PACK = 4
assert BATCH == P * PACK

O_TILE = P
O_TILES = O // O_TILE
LOAD_GROUPS = ((0, 1), (1, 1), (2, 2))
DZ_COLS = O_TILE * OH * OW
X_COLS = C * XH * XW

C_PART = 32
C_PARTS = C // C_PART
WINDOW_BLOCKS = 8
WINDOW = WINDOW_BLOCKS * C_PART
N_MOVING = 2 * WINDOW
assert N_MOVING == 512
WINDOWS = C_PARTS * OH
WINDOWS_COLS = (2 * WINDOWS + 1) * WINDOW

PER_C = OH * OW * KH * KW
PER_H = OW * KH * KW
OUT_COLS = C_PART * PER_C
OUT_BUFS = 8
PSUM_BANKS = 8

FLOPS = 2 * 28 * O * BATCH * C
BYTES = 2 * BATCH * X_COLS + (4 + 2) * BATCH * O * OH * OW + 4 * O * C * PER_C


def tile_locallyconnected2d_v_kernel(tc, x, weight, bias, z, grad_out, out):
    nc = tc.nc
    with ExitStack() as pools:
        keep = pools.enter_context(tc.tile_pool(name="keep", bufs=1))
        work = pools.enter_context(tc.tile_pool(name="work", bufs=2))
        banks = pools.enter_context(tc.psum_pool(name="banks", bufs=PSUM_BANKS))

        pools.enter_context(tc.manual_schedule())

        zero = keep.tile([P, 1], F32)
        nc.vector.memset(zero[:], 0.0)
        out_tiles = []
        for i in range(OUT_BUFS):
            out_tile = keep.tile([P, OUT_COLS], F32, name="out_tile%d" % i)
            nc.scalar.copy(out=out_tile[:], in_=zero[:].to_broadcast([P, OUT_COLS]))
            out_tiles.append(out_tile)
        win_codes = keep.tile([P, WINDOWS_COLS], U32, align_bytes=64)
        win_scales = keep.tile([P, WINDOWS_COLS], U8, align_bytes=64)
        nc.vector.memset(win_codes[:].bitcast(I32), 0)
        nc.vector.memset(win_scales[:].bitcast(I32), 0)
        x_scales = keep.tile([P, X_COLS], U8, align_bytes=64)
        nc.vector.memset(x_scales[:].bitcast(I32), 0)

        x_raw = keep.tile([P, PACK, X_COLS], BF16)
        nc.sync.dma_start(out=x_raw[:], in_=x.rearrange("(p j) c r s -> p j (c r s)", j=PACK))
        g_rows = grad_out.rearrange("(p j) o h w -> p j (o h w)", j=PACK)
        z_rows = z.rearrange("(p j) o h w -> p j (o h w)", j=PACK)
        g_raws = []
        z_raws = []
        for first, count in LOAD_GROUPS:
            dz_cols = slice(first * DZ_COLS, (first + count) * DZ_COLS)
            g_raw = keep.tile([P, PACK, count * DZ_COLS], BF16, name="g_raw%d" % first)
            nc.sync.dma_start(out=g_raw[:], in_=g_rows[:, :, dz_cols])
            z_raw = keep.tile([P, PACK, count * DZ_COLS], F32, name="z_raw%d" % first)
            nc.sync.dma_start(out=z_raw[:], in_=z_rows[:, :, dz_cols])
            for i in range(count):
                g_raws.append(g_raw[:, :, i * DZ_COLS : (i + 1) * DZ_COLS])
                z_raws.append(z_raw[:, :, i * DZ_COLS : (i + 1) * DZ_COLS])

        x_grouped = keep.tile([P, X_COLS * PACK], BF16, align_bytes=64)
        x_codes = keep.tile([P, X_COLS], U32, align_bytes=64)
        x_from = x_raw[:].rearrange("p j (c r s) -> p r c s j", r=XH, s=XW)
        x_to = x_grouped[:].rearrange("p (r s c j) -> p r c s j", r=XH, s=XW, j=PACK)
        row_cols = XW * C

        def quantise_x_row(r):
            cols = slice(r * row_cols, (r + 1) * row_cols)
            nc.vector.quantize_mx(
                out=x_codes[:, cols].bitcast(E4M3_X4),
                scales=x_scales[:, cols],
                in_=x_grouped[:, r * row_cols * PACK : (r + 1) * row_cols * PACK],
            )

        for r in range(XH + 1):
            if r < XH:
                nc.vector.tensor_copy(out=x_to[:, r], in_=x_from[:, r])
            if r > 0:
                quantise_x_row(r - 1)

        def place_row(windows, x_plane, block, h, i):
            r = h + i - 1
            row = x_plane[:, r * XW * C_PARTS * block : (r + 1) * XW * C_PARTS * block]
            behind_first_zeros = windows[:, WINDOW_BLOCKS * block :]
            window_h = behind_first_zeros.rearrange(
                "p (q h e k c) -> p q h e k c", q=C_PARTS, h=OH, e=2, k=WINDOW_BLOCKS
            )[:, :, h, 0]
            nc.vector.tensor_copy(
                out=window_h[:, :, KW * i : KW * i + XW, :],
                in_=row.rearrange("p (s q c) -> p q s c", s=XW, q=C_PARTS),
            )

        for h in range(OH):
            for i in range(KH):
                if 0 <= h + i - 1 < XH:
                    place_row(win_codes[:].bitcast(I32), x_codes[:].bitcast(I32), C_PART, h, i)
                    place_row(win_scales[:].bitcast(I32), x_scales[:].bitcast(I32), C_PART // 4, h, i)

        out_rows = out.rearrange("a (t o) c h w k -> (a t) o (c h w k)", o=O_TILE)
        h_cols = OW * O_TILE
        for t in range(O_TILES):
            slope = z_raws[t]
            nc.vector.tensor_scalar(
                out=slope, in0=z_raws[t], scalar1=0.0, scalar2=NEG_SLOPE, op0=ALU.is_ge, op1=ALU.max
            )
            dz_grouped = work.tile([P, DZ_COLS * PACK], BF16, align_bytes=64)
            dz_codes = work.tile([P, DZ_COLS], U32, align_bytes=64)
            dz_scales = work.tile([P, DZ_COLS], U8, align_bytes=64)
            slope_from = slope.rearrange("p j (o h w) -> p h o j w", h=OH, w=OW)
            g_from = g_raws[t].rearrange("p j (o h w) -> p h o j w", h=OH, w=OW)
            dz_to = dz_grouped[:].rearrange("p (h w o j) -> p h o j w", h=OH, w=OW, j=PACK)
            for h in range(OH + 1):
                if h < OH:
                    nc.vector.tensor_tensor(out=dz_to[:, h], in0=slope_from[:, h], in1=g_from[:, h], op=ALU.mult)
                if h > 0:
                    cols = slice((h - 1) * h_cols, h * h_cols)
                    nc.vector.quantize_mx(
                        out=dz_codes[:, cols].bitcast(E5M2_X4),
                        scales=dz_scales[:, cols],
                        in_=dz_grouped[:, (h - 1) * h_cols * PACK : h * h_cols * PACK],
                    )

            for q in range(C_PARTS):
                out_tile = out_tiles[(t * C_PARTS + q) % OUT_BUFS]
                per_c = out_tile[:].rearrange("p (c f) -> p c f", f=PER_C)
                for h in range(OH):
                    window_start = (2 * (q * OH + h) + 1) * WINDOW
                    bank = banks.tile([P, N_MOVING], F32)
                    for w in range(OW):
                        moving = slice(window_start - w * WINDOW, window_start - w * WINDOW + N_MOVING)
                        stationary = slice((h * OW + w) * O_TILE, (h * OW + w + 1) * O_TILE)
                        nc.tensor.matmul_mx(
                            out=bank[:],
                            lhsT=dz_codes[:, stationary].bitcast(E5M2_X4),
                            lhsT_scale=dz_scales[:, stationary],
                            rhs=win_codes[:, moving].bitcast(E4M3_X4),
                            rhs_scale=win_scales[:, moving],
                            start=(w == 0),
                            stop=(w == OW - 1),
                        )
                    lead = KW * max(0, 1 - h)
                    trail = KW * max(0, h + 2 - XH)
                    to = per_c[:, :, h * PER_H + 1 + lead : (h + 1) * PER_H - 1 - trail]
                    positions = bank[:].rearrange("p (f c) -> p c f", c=C_PART)[:, :, lead : 2 * WINDOW_BLOCKS - trail]
                    if t == O_TILES - 1 and (q * OH + h) % 2 == 1:
                        nc.vector.tensor_copy(out=to, in_=positions)
                    else:
                        nc.scalar.copy(out=to, in_=positions)
                nc.sync.dma_start(out=out_rows[t][:, q * OUT_COLS : (q + 1) * OUT_COLS], in_=out_tile[:])
